import numpy as np
import ml_dtypes


BF16 = ml_dtypes.bfloat16


def bf(x):
    return np.asarray(x, np.float32).astype(BF16)


def f64(x):
    return np.asarray(x).astype(np.float64)


E2M1 = np.array([0.0, 0.5, 1.0, 1.5, 2.0, 3.0, 4.0, 6.0, -0.0, -0.5, -1.0, -1.5, -2.0, -3.0, -4.0, -6.0])


def pack_weight(w, fmt):
    k, n = w.shape
    w = f64(bf(w)).reshape(k // 32, 32, n)
    amax = np.abs(w).max(1)
    if fmt == "e4m3":
        byte = np.frexp(amax)[1] - 1 + 127 - 7
    else:
        mant, ex = np.frexp(amax / 6.0)
        byte = np.where(mant > 0.5, ex, ex - 1) + 127
    byte = np.clip(np.where(amax > 0, byte, 1), 1, 254)
    scaled = (w * np.exp2(127.0 - byte)[:, None, :]).reshape(k, n).astype(np.float32)
    by_word = np.ascontiguousarray(scaled.reshape(k // 512, 128, 4, n).transpose(0, 1, 3, 2))
    if fmt == "e4m3":
        words = by_word.astype(ml_dtypes.float8_e4m3fn).view(np.uint8)
    else:
        c = by_word.astype(ml_dtypes.float4_e2m1fn).view(np.uint8) & 0xF
        words = c[..., 0::2] | (c[..., 1::2] << 4)
    return np.ascontiguousarray(words), np.ascontiguousarray(byte.astype(np.uint8).reshape(k // 512, 16, n))


def unpack_weight(words, scales, fmt):
    g, p, n, _ = words.shape
    if fmt == "e4m3":
        vals = np.ascontiguousarray(words).view(ml_dtypes.float8_e4m3fn).astype(np.float64)
    else:
        nib = np.empty((g, p, n, 4), np.uint8)
        nib[..., 0::2] = words & 0xF
        nib[..., 1::2] = words >> 4
        vals = E2M1[nib]
    vals = vals * np.repeat(np.exp2(scales.astype(np.float64) - 127.0), 8, axis=1)[..., None]
    return vals.transpose(0, 1, 3, 2).reshape(g * 512, n)

def pack4(w):
    words, scales = pack_weight(w, "e2m1")
    return words.reshape(words.shape[0], 128, -1), scales


def unpack4(words, scales):
    return unpack_weight(words.reshape(words.shape[0], 128, -1, 2), scales, "e2m1")


def kspread(k):
    return np.exp2(np.repeat(np.random.randint(-6, 7, k // 32), 32).astype(np.float64))


T, K, E, H, KVH, D = 512, 1024, 3072, 16, 4, 128
EPS = 1e-05


def rmsnorm(x, w):
    var = np.mean(np.square(x), axis=-1, keepdims=True)
    return x * (1.0 / np.sqrt(var + EPS)) * w


def setup_inputs():
    s = kspread(E)
    hidden_states = np.random.standard_normal((T, E)) * s
    hidden_states_words, hidden_states_scales = pack4(np.ascontiguousarray(hidden_states.T))
    wq = np.random.standard_normal((H * D, E)) / np.sqrt(E) / s
    words, scales = pack4(np.ascontiguousarray(wq.T))
    q_norm_w = bf(1.5 + 0.1 * np.random.standard_normal(D))
    return {"hidden_states_words": hidden_states_words,
            "hidden_states_scales": hidden_states_scales,
            "Wq_words": words,
            "Wq_scales": scales,
            "q_norm_w": q_norm_w}


def reference(hidden_states_words, hidden_states_scales, Wq_words, Wq_scales, q_norm_w):
    q = unpack4(hidden_states_words, hidden_states_scales).T @ unpack4(Wq_words, Wq_scales)
    qh = rmsnorm(q.reshape(T, H, D), f64(q_norm_w))
    return qh.transpose(1, 0, 2)

@@ -1,0 +1,162 @@
+from contextlib import ExitStack
+
+import concourse.mybir as mybir
+
+T, K, HEADS, D = 512, 3072, 16, 128
+N_ALL = HEADS * D
+EPS = 1e-05
+FLOPS = 2 * T * K * N_ALL
+
+F32 = mybir.dt.float32
+BF16 = mybir.dt.bfloat16
+I32 = mybir.dt.int32
+U8 = mybir.dt.uint8
+FP4X4 = mybir.dt.float4_e2m1fn_x4
+ACT = mybir.ActivationFunctionType
+ALU = mybir.AluOpType
+
+P = 128
+PASSES = K // 512
+CHUNK = 512
+CHUNKS = N_ALL // CHUNK
+TOKEN_TILES = T // P
+WARM_UPS = 9
+
+
+def tile_combcrossattention_pa_kernel(tc, x_words, x_scales, w_words, w_scales, gain, out):
+    nc = tc.nc
+
+    with ExitStack() as ctx:
+        keep = ctx.enter_context(tc.tile_pool(name="keep", bufs=1))
+        work = ctx.enter_context(tc.tile_pool(name="work", bufs=4))
+        results = ctx.enter_context(tc.tile_pool(name="results", bufs=8))
+        psum = ctx.enter_context(tc.psum_pool(name="psum", bufs=8))
+        ctx.enter_context(tc.manual_schedule())
+
+        xc = keep.tile([P, PASSES, 2 * T], U8, align_bytes=256)
+        xs = keep.tile([P, PASSES, T], U8, align_bytes=256)
+        wc = []
+        for c in range(CHUNKS):
+            codes = keep.tile([P, PASSES, 2 * CHUNK], U8, align_bytes=256, name=f"wc{c}")
+            wc.append(codes)
+        ws_first = keep.tile([P, PASSES, CHUNK], U8, align_bytes=256)
+        ws_rest = keep.tile([P, PASSES, N_ALL - CHUNK], U8, align_bytes=256)
+
+        zeros = keep.tile([P, 512], BF16)
+        ones = keep.tile([P, P], BF16)
+        gain_row = keep.tile([P, D], BF16)
+        gain_all = keep.tile([P, D], F32)
+        one = keep.tile([P, 1], F32)
+        one_out = keep.tile([P, 1], F32)
+
+        def load_x(g0, g1):
+            nc.sync.dma_start(
+                out=xc[:, g0:g1, :].bitcast(I32),
+                in_=x_words[g0:g1, :, :].rearrange("g p b -> p g b").bitcast(I32),
+            )
+
+        def load_w(c, g0, g1):
+            nc.sync.dma_start(
+                out=wc[c][:, g0:g1, :].bitcast(I32),
+                in_=w_words[g0:g1, :, 2 * CHUNK * c : 2 * CHUNK * (c + 1)].rearrange("g p b -> p g b").bitcast(I32),
+            )
+
+        def load_scales(plane, src):
+            for q in range(4):
+                nc.sync.dma_start(
+                    out=plane[32 * q : 32 * q + 4, :, :].bitcast(I32),
+                    in_=src[:, 4 * q : 4 * q + 4, :].rearrange("g r n -> r g n").bitcast(I32),
+                )
+
+        nc.gpsimd.memset(zeros[:], 0.0)
+        nc.gpsimd.memset(gain_row[:], 0.0)
+        nc.gpsimd.dma_start(out=gain_row[0:1, :], in_=gain.unsqueeze(0))
+        nc.gpsimd.memset(one[:], 1.0)
+        nc.gpsimd.memset(ones[:], 1.0)
+        nc.vector.memset(xs[:].bitcast(I32), 0)
+        nc.vector.memset(ws_first[:].bitcast(I32), 0)
+        nc.vector.memset(ws_rest[:].bitcast(I32), 0)
+        nc.scalar.activation(out=one_out[:], in_=one[:], func=ACT.Abs_reciprocal_sqrt, bias=EPS, scale=1.0 / D)
+
+        load_x(0, 1)
+        load_w(0, 0, 1)
+        load_scales(xs, x_scales)
+        load_scales(ws_first, w_scales[:, :, 0:CHUNK])
+        load_x(1, 3)
+        load_w(0, 1, 3)
+        load_x(3, 6)
+        load_w(0, 3, 6)
+        load_scales(ws_rest, w_scales[:, :, CHUNK:N_ALL])
+        for c in range(1, CHUNKS):
+            load_w(c, 0, PASSES)
+
+        warm = psum.tile([P, 512], F32, tag="acc", name="warm")
+        for _ in range(WARM_UPS):
+            nc.tensor.matmul(warm[:], zeros[:, 0:P], zeros[:], start=True, stop=True)
+
+        def one_pass(acc, t, n0, width, g):
+            c = n0 // CHUNK
+            n_in = n0 - CHUNK * c
+            plane = ws_first[:, g, n0 : n0 + width] if c == 0 else ws_rest[:, g, n0 - CHUNK : n0 - CHUNK + width]
+            nc.tensor.matmul_mx(
+                out=acc[:, 0:width],
+                lhsT=xc[:, g, 2 * P * t : 2 * P * (t + 1)].bitcast(FP4X4),
+                lhsT_scale=xs[:, g, P * t : P * (t + 1)],
+                rhs=wc[c][:, g, 2 * n_in : 2 * (n_in + width)].bitcast(FP4X4),
+                rhs_scale=plane,
+                start=(g == 0),
+                stop=(g == PASSES - 1),
+            )
+
+        def finish(acc, t, n0, width):
+            heads = width // D
+            square = work.tile([P, D], BF16, name="square")
+            sums = work.tile([P, 4], F32, name="sums")
+            factor = work.tile([P, 4], F32, name="factor")
+            res = results.tile([P, 4, D], F32, name="res")
+            for h in range(heads):
+                nc.scalar.activation(
+                    out=square[:], in_=acc[:, D * h : D * (h + 1)], func=ACT.Square, accum_out=sums[:, h : h + 1]
+                )
+            nc.scalar.activation(
+                out=factor[:, 0:heads], in_=sums[:, 0:heads], func=ACT.Abs_reciprocal_sqrt, bias=EPS, scale=1.0 / D
+            )
+            for h in range(heads):
+                nc.vector.scalar_tensor_tensor(
+                    out=res[:, h, :],
+                    in0=acc[:, D * h : D * (h + 1)],
+                    scalar=factor[:, h : h + 1],
+                    in1=gain_all[:],
+                    op0=ALU.mult,
+                    op1=ALU.mult,
+                )
+            h0 = n0 // D
+            nc.sync.dma_start(
+                out=out[h0 : h0 + heads, P * t : P * (t + 1), :].rearrange("h p d -> p h d"), in_=res[:, 0:heads, :]
+            )
+
+        first = []
+        for t in range(TOKEN_TILES):
+            acc = psum.tile([P, CHUNK], F32, tag="acc", name="acc")
+            first.append(acc)
+        for g in range(PASSES):
+            for t in range(TOKEN_TILES):
+                one_pass(first[t], t, 0, CHUNK, g)
+            if g == 1:
+                nc.tensor.matmul(warm[:, 0:D], ones[:], gain_row[:], start=True, stop=True)
+                nc.vector.tensor_copy(out=gain_all[:], in_=warm[:, 0:D])
+        for t in range(TOKEN_TILES):
+            finish(first[t], t, 0, CHUNK)
+
+        pieces = []
+        for c in range(1, CHUNKS):
+            for t in range(TOKEN_TILES):
+                if c == CHUNKS - 1 and t == TOKEN_TILES - 1:
+                    pieces.extend([(t, CHUNK * c, 256), (t, CHUNK * c + 256, 128), (t, CHUNK * c + 384, 128)])
+                else:
+                    pieces.append((t, CHUNK * c, CHUNK))
+        for t, n0, width in pieces:
+            acc = psum.tile([P, CHUNK], F32, tag="acc", name="acc")
+            for g in range(PASSES):
+                one_pass(acc, t, n0, width, g)
+            finish(acc, t, n0, width)

@@ -39,8 +39,10 @@ def tile_combcrossattention_pa_kernel(tc, x_words, x_scales, w_words, w_scales, 
         for c in range(CHUNKS):
             codes = keep.tile([P, PASSES, 2 * CHUNK], U8, align_bytes=256, name=f"wc{c}")
             wc.append(codes)
-        ws_first = keep.tile([P, PASSES, CHUNK], U8, align_bytes=256)
-        ws_rest = keep.tile([P, PASSES, N_ALL - CHUNK], U8, align_bytes=256)
+        ws = []
+        for c in range(CHUNKS):
+            plane = keep.tile([P, PASSES, CHUNK], U8, align_bytes=256, name=f"ws{c}")
+            ws.append(plane)
 
         zeros = keep.tile([P, 512], BF16)
         ones = keep.tile([P, P], BF16)
@@ -62,10 +64,10 @@ def tile_combcrossattention_pa_kernel(tc, x_words, x_scales, w_words, w_scales, 
             )
 
         def load_scales(plane, src):
-            for q in range(4):
+            for r in range(4):
                 nc.sync.dma_start(
-                    out=plane[32 * q : 32 * q + 4, :, :].bitcast(I32),
-                    in_=src[:, 4 * q : 4 * q + 4, :].rearrange("g r n -> r g n").bitcast(I32),
+                    out=plane[r:P:32, :, :].bitcast(I32),
+                    in_=src[:, r:16:4, :].rearrange("g q n -> q g n").bitcast(I32),
                 )
 
         nc.gpsimd.memset(zeros[:], 0.0)
@@ -74,20 +76,20 @@ def tile_combcrossattention_pa_kernel(tc, x_words, x_scales, w_words, w_scales, 
         nc.gpsimd.memset(one[:], 1.0)
         nc.gpsimd.memset(ones[:], 1.0)
         nc.vector.memset(xs[:].bitcast(I32), 0)
-        nc.vector.memset(ws_first[:].bitcast(I32), 0)
-        nc.vector.memset(ws_rest[:].bitcast(I32), 0)
+        for c in range(CHUNKS):
+            nc.vector.memset(ws[c][:].bitcast(I32), 0)
         nc.scalar.activation(out=one_out[:], in_=one[:], func=ACT.Abs_reciprocal_sqrt, bias=EPS, scale=1.0 / D)
 
         load_x(0, 1)
         load_w(0, 0, 1)
         load_scales(xs, x_scales)
-        load_scales(ws_first, w_scales[:, :, 0:CHUNK])
+        load_scales(ws[0], w_scales[:, :, 0:CHUNK])
         load_x(1, 3)
         load_w(0, 1, 3)
         load_x(3, 6)
         load_w(0, 3, 6)
-        load_scales(ws_rest, w_scales[:, :, CHUNK:N_ALL])
         for c in range(1, CHUNKS):
+            load_scales(ws[c], w_scales[:, :, CHUNK * c : CHUNK * (c + 1)])
             load_w(c, 0, PASSES)
 
         warm = psum.tile([P, 512], F32, tag="acc", name="warm")
@@ -97,13 +99,12 @@ def tile_combcrossattention_pa_kernel(tc, x_words, x_scales, w_words, w_scales, 
         def one_pass(acc, t, n0, width, g):
             c = n0 // CHUNK
             n_in = n0 - CHUNK * c
-            plane = ws_first[:, g, n0 : n0 + width] if c == 0 else ws_rest[:, g, n0 - CHUNK : n0 - CHUNK + width]
             nc.tensor.matmul_mx(
                 out=acc[:, 0:width],
                 lhsT=xc[:, g, 2 * P * t : 2 * P * (t + 1)].bitcast(FP4X4),
                 lhsT_scale=xs[:, g, P * t : P * (t + 1)],
                 rhs=wc[c][:, g, 2 * n_in : 2 * (n_in + width)].bitcast(FP4X4),
-                rhs_scale=plane,
+                rhs_scale=ws[c][:, g, n_in : n_in + width],
                 start=(g == 0),
                 stop=(g == PASSES - 1),
             )

@@ -20,7 +20,7 @@ PASSES = K // 512
 CHUNK = 512
 CHUNKS = N_ALL // CHUNK
 TOKEN_TILES = T // P
-WARM_UPS = 9
+WARM_UPS = 7
 
 
 def tile_combcrossattention_pa_kernel(tc, x_words, x_scales, w_words, w_scales, gain, out):
@@ -48,7 +48,6 @@ def tile_combcrossattention_pa_kernel(tc, x_words, x_scales, w_words, w_scales, 
         ones = keep.tile([P, P], BF16)
         gain_row = keep.tile([P, D], BF16)
         gain_all = keep.tile([P, D], F32)
-        one = keep.tile([P, 1], F32)
         one_out = keep.tile([P, 1], F32)
 
         def load_x(g0, g1):
@@ -70,15 +69,14 @@ def tile_combcrossattention_pa_kernel(tc, x_words, x_scales, w_words, w_scales, 
                     in_=src[:, r:16:4, :].rearrange("g q n -> q g n").bitcast(I32),
                 )
 
-        nc.gpsimd.memset(zeros[:], 0.0)
-        nc.gpsimd.memset(gain_row[:], 0.0)
-        nc.gpsimd.dma_start(out=gain_row[0:1, :], in_=gain.unsqueeze(0))
-        nc.gpsimd.memset(one[:], 1.0)
-        nc.gpsimd.memset(ones[:], 1.0)
+        nc.vector.memset(zeros[:], 0.0)
         nc.vector.memset(xs[:].bitcast(I32), 0)
         for c in range(CHUNKS):
             nc.vector.memset(ws[c][:].bitcast(I32), 0)
-        nc.scalar.activation(out=one_out[:], in_=one[:], func=ACT.Abs_reciprocal_sqrt, bias=EPS, scale=1.0 / D)
+        nc.vector.memset(ones[:], 1.0)
+        nc.vector.memset(gain_row[:], 0.0)
+        nc.scalar.activation(out=one_out[:], in_=zeros[:, 0:1], func=ACT.Abs_reciprocal_sqrt, bias=EPS, scale=1.0 / D)
+        nc.gpsimd.dma_start(out=gain_row[0:1, :], in_=gain.unsqueeze(0))
 
         load_x(0, 1)
         load_w(0, 0, 1)
@@ -143,9 +141,8 @@ def tile_combcrossattention_pa_kernel(tc, x_words, x_scales, w_words, w_scales, 
         for g in range(PASSES):
             for t in range(TOKEN_TILES):
                 one_pass(first[t], t, 0, CHUNK, g)
-            if g == 1:
-                nc.tensor.matmul(warm[:, 0:D], ones[:], gain_row[:], start=True, stop=True)
-                nc.vector.tensor_copy(out=gain_all[:], in_=warm[:, 0:D])
+        nc.tensor.matmul(warm[:, 0:D], ones[:], gain_row[:], start=True, stop=True)
+        nc.vector.tensor_copy(out=gain_all[:], in_=warm[:, 0:D])
         for t in range(TOKEN_TILES):
             finish(first[t], t, 0, CHUNK)
 

@@ -20,7 +20,7 @@ PASSES = K // 512
 CHUNK = 512
 CHUNKS = N_ALL // CHUNK
 TOKEN_TILES = T // P
-WARM_UPS = 7
+WARM_UPS = 10
 
 
 def tile_combcrossattention_pa_kernel(tc, x_words, x_scales, w_words, w_scales, gain, out):
@@ -69,14 +69,14 @@ def tile_combcrossattention_pa_kernel(tc, x_words, x_scales, w_words, w_scales, 
                     in_=src[:, r:16:4, :].rearrange("g q n -> q g n").bitcast(I32),
                 )
 
+        nc.gpsimd.memset(gain_row[:], 0.0)
+        nc.gpsimd.dma_start(out=gain_row[0:1, :], in_=gain.unsqueeze(0))
+        nc.gpsimd.memset(ones[:], 1.0)
         nc.vector.memset(zeros[:], 0.0)
         nc.vector.memset(xs[:].bitcast(I32), 0)
         for c in range(CHUNKS):
             nc.vector.memset(ws[c][:].bitcast(I32), 0)
-        nc.vector.memset(ones[:], 1.0)
-        nc.vector.memset(gain_row[:], 0.0)
         nc.scalar.activation(out=one_out[:], in_=zeros[:, 0:1], func=ACT.Abs_reciprocal_sqrt, bias=EPS, scale=1.0 / D)
-        nc.gpsimd.dma_start(out=gain_row[0:1, :], in_=gain.unsqueeze(0))
 
         load_x(0, 1)
         load_w(0, 0, 1)
@@ -107,19 +107,31 @@ def tile_combcrossattention_pa_kernel(tc, x_words, x_scales, w_words, w_scales, 
                 stop=(g == PASSES - 1),
             )
 
-        def finish(acc, t, n0, width):
+        def factors(acc, width):
             heads = width // D
-            square = work.tile([P, D], BF16, name="square")
+            wide = 2 if heads == 4 else 0
+            square = work.tile([P, 4, D], F32, name="square")
             sums = work.tile([P, 4], F32, name="sums")
             factor = work.tile([P, 4], F32, name="factor")
-            res = results.tile([P, 4, D], F32, name="res")
-            for h in range(heads):
+            if wide:
                 nc.scalar.activation(
-                    out=square[:], in_=acc[:, D * h : D * (h + 1)], func=ACT.Square, accum_out=sums[:, h : h + 1]
+                    out=square[:, 0:wide, :].rearrange("p h d -> p (h d)"), in_=acc[:, 0 : D * wide], func=ACT.Square
+                )
+                nc.vector.tensor_reduce(
+                    out=sums[:, 0:wide], in_=square[:, 0:wide, :], op=ALU.add, axis=mybir.AxisListType.X
+                )
+            for h in range(wide, heads):
+                nc.scalar.activation(
+                    out=square[:, h, :], in_=acc[:, D * h : D * (h + 1)], func=ACT.Square, accum_out=sums[:, h : h + 1]
                 )
             nc.scalar.activation(
                 out=factor[:, 0:heads], in_=sums[:, 0:heads], func=ACT.Abs_reciprocal_sqrt, bias=EPS, scale=1.0 / D
             )
+            return factor
+
+        def apply(acc, factor, t, n0, width):
+            heads = width // D
+            res = results.tile([P, 4, D], F32, name="res")
             for h in range(heads):
                 nc.vector.scalar_tensor_tensor(
                     out=res[:, h, :],
@@ -138,23 +150,31 @@ def tile_combcrossattention_pa_kernel(tc, x_words, x_scales, w_words, w_scales, 
         for t in range(TOKEN_TILES):
             acc = psum.tile([P, CHUNK], F32, tag="acc", name="acc")
             first.append(acc)
-        for g in range(PASSES):
+        for g in range(3):
             for t in range(TOKEN_TILES):
                 one_pass(first[t], t, 0, CHUNK, g)
         nc.tensor.matmul(warm[:, 0:D], ones[:], gain_row[:], start=True, stop=True)
         nc.vector.tensor_copy(out=gain_all[:], in_=warm[:, 0:D])
-        for t in range(TOKEN_TILES):
-            finish(first[t], t, 0, CHUNK)
 
         pieces = []
-        for c in range(1, CHUNKS):
+        for c in range(CHUNKS):
             for t in range(TOKEN_TILES):
                 if c == CHUNKS - 1 and t == TOKEN_TILES - 1:
                     pieces.extend([(t, CHUNK * c, 256), (t, CHUNK * c + 256, 128), (t, CHUNK * c + 384, 128)])
                 else:
                     pieces.append((t, CHUNK * c, CHUNK))
+        waiting = []
         for t, n0, width in pieces:
-            acc = psum.tile([P, CHUNK], F32, tag="acc", name="acc")
-            for g in range(PASSES):
+            if n0 == 0:
+                acc = first[t]
+            else:
+                acc = psum.tile([P, CHUNK], F32, tag="acc", name="acc")
+            for g in range(3 if n0 == 0 else 0, PASSES):
                 one_pass(acc, t, n0, width, g)
-            finish(acc, t, n0, width)
+            if width < CHUNK and waiting:
+                apply(*waiting.pop())
+            factor = factors(acc, width)
+            if waiting:
+                apply(*waiting.pop())
+            waiting.append((acc, factor, t, n0, width))
+        apply(*waiting.pop())

from contextlib import ExitStack

import concourse.mybir as mybir

T, K, HEADS, D = 512, 3072, 16, 128
N_ALL = HEADS * D
EPS = 1e-05
FLOPS = 2 * T * K * N_ALL

F32 = mybir.dt.float32
BF16 = mybir.dt.bfloat16
I32 = mybir.dt.int32
U8 = mybir.dt.uint8
FP4X4 = mybir.dt.float4_e2m1fn_x4
ACT = mybir.ActivationFunctionType
ALU = mybir.AluOpType

P = 128
PASSES = K // 512
CHUNK = 512
CHUNKS = N_ALL // CHUNK
TOKEN_TILES = T // P
WARM_UPS = 10


def tile_combcrossattention_pa_kernel(tc, x_words, x_scales, w_words, w_scales, gain, out):
    nc = tc.nc

    with ExitStack() as ctx:
        keep = ctx.enter_context(tc.tile_pool(name="keep", bufs=1))
        work = ctx.enter_context(tc.tile_pool(name="work", bufs=4))
        results = ctx.enter_context(tc.tile_pool(name="results", bufs=8))
        psum = ctx.enter_context(tc.psum_pool(name="psum", bufs=8))
        ctx.enter_context(tc.manual_schedule())

        xc = keep.tile([P, PASSES, 2 * T], U8, align_bytes=256)
        xs = keep.tile([P, PASSES, T], U8, align_bytes=256)
        wc = []
        for c in range(CHUNKS):
            codes = keep.tile([P, PASSES, 2 * CHUNK], U8, align_bytes=256, name=f"wc{c}")
            wc.append(codes)
        ws = []
        for c in range(CHUNKS):
            plane = keep.tile([P, PASSES, CHUNK], U8, align_bytes=256, name=f"ws{c}")
            ws.append(plane)

        zeros = keep.tile([P, 512], BF16)
        ones = keep.tile([P, P], BF16)
        gain_row = keep.tile([P, D], BF16)
        gain_all = keep.tile([P, D], F32)
        one_out = keep.tile([P, 1], F32)

        def load_x(g0, g1):
            nc.sync.dma_start(
                out=xc[:, g0:g1, :].bitcast(I32),
                in_=x_words[g0:g1, :, :].rearrange("g p b -> p g b").bitcast(I32),
            )

        def load_w(c, g0, g1):
            nc.sync.dma_start(
                out=wc[c][:, g0:g1, :].bitcast(I32),
                in_=w_words[g0:g1, :, 2 * CHUNK * c : 2 * CHUNK * (c + 1)].rearrange("g p b -> p g b").bitcast(I32),
            )

        def load_scales(plane, src):
            for r in range(4):
                nc.sync.dma_start(
                    out=plane[r:P:32, :, :].bitcast(I32),
                    in_=src[:, r:16:4, :].rearrange("g q n -> q g n").bitcast(I32),
                )

        nc.gpsimd.memset(gain_row[:], 0.0)
        nc.gpsimd.dma_start(out=gain_row[0:1, :], in_=gain.unsqueeze(0))
        nc.gpsimd.memset(ones[:], 1.0)
        nc.vector.memset(zeros[:], 0.0)
        nc.vector.memset(xs[:].bitcast(I32), 0)
        for c in range(CHUNKS):
            nc.vector.memset(ws[c][:].bitcast(I32), 0)
        nc.scalar.activation(out=one_out[:], in_=zeros[:, 0:1], func=ACT.Abs_reciprocal_sqrt, bias=EPS, scale=1.0 / D)

        load_x(0, 1)
        load_w(0, 0, 1)
        load_scales(xs, x_scales)
        load_scales(ws[0], w_scales[:, :, 0:CHUNK])
        load_x(1, 3)
        load_w(0, 1, 3)
        load_x(3, 6)
        load_w(0, 3, 6)
        for c in range(1, CHUNKS):
            load_scales(ws[c], w_scales[:, :, CHUNK * c : CHUNK * (c + 1)])
            load_w(c, 0, PASSES)

        warm = psum.tile([P, 512], F32, tag="acc", name="warm")
        for _ in range(WARM_UPS):
            nc.tensor.matmul(warm[:], zeros[:, 0:P], zeros[:], start=True, stop=True)

        def one_pass(acc, t, n0, width, g):
            c = n0 // CHUNK
            n_in = n0 - CHUNK * c
            nc.tensor.matmul_mx(
                out=acc[:, 0:width],
                lhsT=xc[:, g, 2 * P * t : 2 * P * (t + 1)].bitcast(FP4X4),
                lhsT_scale=xs[:, g, P * t : P * (t + 1)],
                rhs=wc[c][:, g, 2 * n_in : 2 * (n_in + width)].bitcast(FP4X4),
                rhs_scale=ws[c][:, g, n_in : n_in + width],
                start=(g == 0),
                stop=(g == PASSES - 1),
            )

        def factors(acc, width):
            heads = width // D
            wide = 2 if heads == 4 else 0
            square = work.tile([P, 4, D], F32, name="square")
            sums = work.tile([P, 4], F32, name="sums")
            factor = work.tile([P, 4], F32, name="factor")
            if wide:
                nc.scalar.activation(
                    out=square[:, 0:wide, :].rearrange("p h d -> p (h d)"), in_=acc[:, 0 : D * wide], func=ACT.Square
                )
                nc.vector.tensor_reduce(
                    out=sums[:, 0:wide], in_=square[:, 0:wide, :], op=ALU.add, axis=mybir.AxisListType.X
                )
            for h in range(wide, heads):
                nc.scalar.activation(
                    out=square[:, h, :], in_=acc[:, D * h : D * (h + 1)], func=ACT.Square, accum_out=sums[:, h : h + 1]
                )
            nc.scalar.activation(
                out=factor[:, 0:heads], in_=sums[:, 0:heads], func=ACT.Abs_reciprocal_sqrt, bias=EPS, scale=1.0 / D
            )
            return factor

        def apply(acc, factor, t, n0, width):
            heads = width // D
            res = results.tile([P, 4, D], F32, name="res")
            for h in range(heads):
                nc.vector.scalar_tensor_tensor(
                    out=res[:, h, :],
                    in0=acc[:, D * h : D * (h + 1)],
                    scalar=factor[:, h : h + 1],
                    in1=gain_all[:],
                    op0=ALU.mult,
                    op1=ALU.mult,
                )
            h0 = n0 // D
            nc.sync.dma_start(
                out=out[h0 : h0 + heads, P * t : P * (t + 1), :].rearrange("h p d -> p h d"), in_=res[:, 0:heads, :]
            )

        first = []
        for t in range(TOKEN_TILES):
            acc = psum.tile([P, CHUNK], F32, tag="acc", name="acc")
            first.append(acc)
        for g in range(3):
            for t in range(TOKEN_TILES):
                one_pass(first[t], t, 0, CHUNK, g)
        nc.tensor.matmul(warm[:, 0:D], ones[:], gain_row[:], start=True, stop=True)
        nc.vector.tensor_copy(out=gain_all[:], in_=warm[:, 0:D])

        pieces = []
        for c in range(CHUNKS):
            for t in range(TOKEN_TILES):
                if c == CHUNKS - 1 and t == TOKEN_TILES - 1:
                    pieces.extend([(t, CHUNK * c, 256), (t, CHUNK * c + 256, 128), (t, CHUNK * c + 384, 128)])
                else:
                    pieces.append((t, CHUNK * c, CHUNK))
        waiting = []
        for t, n0, width in pieces:
            if n0 == 0:
                acc = first[t]
            else:
                acc = psum.tile([P, CHUNK], F32, tag="acc", name="acc")
            for g in range(3 if n0 == 0 else 0, PASSES):
                one_pass(acc, t, n0, width, g)
            if width < CHUNK and waiting:
                apply(*waiting.pop())
            factor = factors(acc, width)
            if waiting:
                apply(*waiting.pop())
            waiting.append((acc, factor, t, n0, width))
        apply(*waiting.pop())
